import numpy as np
import ml_dtypes

BF16 = ml_dtypes.bfloat16


def bf(x):
    return np.asarray(x, np.float32).astype(BF16)


def f32(x):
    return np.asarray(x, np.float32)


def f64(x):
    return np.asarray(x).astype(np.float64)


def striped(idx):
    return np.tile(idx.reshape(-1, 16).T, (8, 1))


V, D, N = 256, 128, 128
FREQ = 60.0


def coherence_mask(n):
    t = np.linspace(0.0, 1.0, n).astype(np.float32)
    ph = np.float32(FREQ * 2.0 * np.pi) * t
    d = ph[:, None] - ph[None, :]
    return f32(1.0 / (1.0 + np.exp(-np.cos(f64(d)))))


def setup_inputs():
    return {"table": bf(np.random.standard_normal((D, V))), "w1": bf(4.5 * np.random.standard_normal((D, D)) / np.sqrt(D)), "fw1": bf(4.5 * np.random.standard_normal((D, D)) / np.sqrt(D)), "b1": f32(0.1 * np.random.standard_normal((D, 1))), "mask": coherence_mask(N), "offs": striped(np.random.permutation(np.tile(np.arange(V), 2))[:N])}


def reference(table, w1, fw1, b1, mask, offs):
    idx = offs[:16].T.reshape(-1)
    y = (f64(w1) + f64(fw1)).T @ f64(table)[:, idx]
    return np.tanh(y @ f64(mask) / N + f64(b1))

@@ -1,0 +1,57 @@
+import concourse.mybir as mybir
+from concourse.masks import make_identity
+
+BF16, F32, U16 = mybir.dt.bfloat16, mybir.dt.float32, mybir.dt.uint16
+
+D = 128
+V = 256
+N = 128
+
+FLOPS = 2 * D * D * N + 2 * D * N * N
+
+
+def tile_neuronsv2textclassifier_kernel(tc, table, w1, fw1, b1, mask, offs, out):
+    nc = tc.nc
+    with (
+        tc.tile_pool(name="held", bufs=1) as held,
+        tc.psum_pool(name="psum", bufs=1) as psum,
+    ):
+        offsets = held.tile([D, N // 16], U16, name="offsets")
+        nc.sync.dma_start(offsets[:], offs)
+        table_sb = held.tile([D, V], BF16, name="table_sb")
+        nc.sync.dma_start(table_sb[:], table)
+        w1_sb = held.tile([D, D], BF16, name="w1_sb")
+        nc.scalar.dma_start(w1_sb[:], w1)
+        fw1_sb = held.tile([D, D], BF16, name="fw1_sb")
+        nc.scalar.dma_start(fw1_sb[:], fw1)
+        mask_f32 = held.tile([N, N], F32, name="mask_f32")
+        nc.gpsimd.dma_start(mask_f32[:], mask)
+        b1_sb = held.tile([D, 1], F32, name="b1_sb")
+        nc.gpsimd.dma_start(b1_sb[:], b1)
+
+        identity = held.tile([D, D], BF16, name="identity")
+        make_identity(nc, identity[:])
+        mask_bf = held.tile([N, N], BF16, name="mask_bf")
+        nc.gpsimd.tensor_copy(mask_bf[:], mask_f32[:])
+
+        w_sum = held.tile([D, D], BF16, name="w_sum")
+        nc.vector.tensor_tensor(w_sum[:], w1_sb[:], fw1_sb[:], mybir.AluOpType.add)
+
+        y_ps = psum.tile([D, N], F32, name="y_ps")
+        nc.tensor.matmul(y_ps[:], w_sum[:], table_sb[:].indirect(offsets[:]), start=True, stop=True)
+        y_bf = held.tile([D, N], BF16, name="y_bf")
+        nc.vector.tensor_copy(y_bf[:], y_ps[:])
+
+        yT_ps = psum.tile([N, D], BF16, name="yT_ps")
+        nc.tensor.transpose(yT_ps[:], y_bf[:], identity[:])
+        yT_bf = held.tile([N, D], BF16, name="yT_bf")
+        nc.vector.tensor_copy(yT_bf[:], yT_ps[:])
+
+        mixed_ps = psum.tile([D, N], F32, name="mixed_ps")
+        nc.tensor.matmul(mixed_ps[:], yT_bf[:], mask_bf[:], start=True, stop=True)
+
+        out_sb = held.tile([D, N], F32, name="out_sb")
+        nc.scalar.activation(
+            out_sb[:], mixed_ps[:], mybir.ActivationFunctionType.Tanh, bias=b1_sb[:], scale=1.0 / N
+        )
+        nc.sync.dma_start(out, out_sb[:])

@@ -29,6 +29,10 @@ def tile_neuronsv2textclassifier_kernel(tc, table, w1, fw1, b1, mask, offs, out)
         b1_sb = held.tile([D, 1], F32, name="b1_sb")
         nc.gpsimd.dma_start(b1_sb[:], b1)
 
+        scratch = held.tile([D, 1], F32, name="scratch")
+        nc.vector.memset(scratch[:], 0.0)
+        nc.scalar.activation(scratch[:], scratch[:], mybir.ActivationFunctionType.Tanh)
+
         identity = held.tile([D, D], BF16, name="identity")
         make_identity(nc, identity[:])
         mask_bf = held.tile([N, N], BF16, name="mask_bf")

@@ -25,9 +25,9 @@ def tile_neuronsv2textclassifier_kernel(tc, table, w1, fw1, b1, mask, offs, out)
         fw1_sb = held.tile([D, D], BF16, name="fw1_sb")
         nc.scalar.dma_start(fw1_sb[:], fw1)
         mask_f32 = held.tile([N, N], F32, name="mask_f32")
-        nc.gpsimd.dma_start(mask_f32[:], mask)
+        nc.sync.dma_start(mask_f32[:], mask)
         b1_sb = held.tile([D, 1], F32, name="b1_sb")
-        nc.gpsimd.dma_start(b1_sb[:], b1)
+        nc.scalar.dma_start(b1_sb[:], b1)
 
         scratch = held.tile([D, 1], F32, name="scratch")
         nc.vector.memset(scratch[:], 0.0)
@@ -35,8 +35,6 @@ def tile_neuronsv2textclassifier_kernel(tc, table, w1, fw1, b1, mask, offs, out)
 
         identity = held.tile([D, D], BF16, name="identity")
         make_identity(nc, identity[:])
-        mask_bf = held.tile([N, N], BF16, name="mask_bf")
-        nc.gpsimd.tensor_copy(mask_bf[:], mask_f32[:])
 
         w_sum = held.tile([D, D], BF16, name="w_sum")
         nc.vector.tensor_tensor(w_sum[:], w1_sb[:], fw1_sb[:], mybir.AluOpType.add)
@@ -48,6 +46,8 @@ def tile_neuronsv2textclassifier_kernel(tc, table, w1, fw1, b1, mask, offs, out)
 
         yT_ps = psum.tile([N, D], BF16, name="yT_ps")
         nc.tensor.transpose(yT_ps[:], y_bf[:], identity[:])
+        mask_bf = held.tile([N, N], BF16, name="mask_bf")
+        nc.vector.tensor_copy(mask_bf[:], mask_f32[:])
         yT_bf = held.tile([N, D], BF16, name="yT_bf")
         nc.vector.tensor_copy(yT_bf[:], yT_ps[:])
 

@@ -7,6 +7,9 @@ D = 128
 V = 256
 N = 128
 
+BANK = 512
+WARMING_MATMULS = 4
+
 FLOPS = 2 * D * D * N + 2 * D * N * N
 
 
@@ -32,6 +35,12 @@ def tile_neuronsv2textclassifier_kernel(tc, table, w1, fw1, b1, mask, offs, out)
         scratch = held.tile([D, 1], F32, name="scratch")
         nc.vector.memset(scratch[:], 0.0)
         nc.scalar.activation(scratch[:], scratch[:], mybir.ActivationFunctionType.Tanh)
+
+        zeros = held.tile([D, BANK], BF16, name="zeros")
+        nc.vector.memset(zeros[:], 0.0)
+        unused_ps = psum.tile([D, BANK], F32, name="unused_ps")
+        for _ in range(WARMING_MATMULS):
+            nc.tensor.matmul(unused_ps[:], zeros[:, 0:D], zeros[:], start=True, stop=True)
 
         identity = held.tile([D, D], BF16, name="identity")
         make_identity(nc, identity[:])

@@ -7,9 +7,6 @@ D = 128
 V = 256
 N = 128
 
-BANK = 512
-WARMING_MATMULS = 4
-
 FLOPS = 2 * D * D * N + 2 * D * N * N
 
 
@@ -19,14 +16,14 @@ def tile_neuronsv2textclassifier_kernel(tc, table, w1, fw1, b1, mask, offs, out)
         tc.tile_pool(name="held", bufs=1) as held,
         tc.psum_pool(name="psum", bufs=1) as psum,
     ):
-        offsets = held.tile([D, N // 16], U16, name="offsets")
-        nc.sync.dma_start(offsets[:], offs)
-        table_sb = held.tile([D, V], BF16, name="table_sb")
-        nc.sync.dma_start(table_sb[:], table)
         w1_sb = held.tile([D, D], BF16, name="w1_sb")
         nc.scalar.dma_start(w1_sb[:], w1)
         fw1_sb = held.tile([D, D], BF16, name="fw1_sb")
-        nc.scalar.dma_start(fw1_sb[:], fw1)
+        nc.sync.dma_start(fw1_sb[:], fw1)
+        table_sb = held.tile([D, V], BF16, name="table_sb")
+        nc.scalar.dma_start(table_sb[:], table)
+        offsets = held.tile([D, N // 16], U16, name="offsets")
+        nc.sync.dma_start(offsets[:], offs)
         mask_f32 = held.tile([N, N], F32, name="mask_f32")
         nc.sync.dma_start(mask_f32[:], mask)
         b1_sb = held.tile([D, 1], F32, name="b1_sb")
@@ -35,12 +32,6 @@ def tile_neuronsv2textclassifier_kernel(tc, table, w1, fw1, b1, mask, offs, out)
         scratch = held.tile([D, 1], F32, name="scratch")
         nc.vector.memset(scratch[:], 0.0)
         nc.scalar.activation(scratch[:], scratch[:], mybir.ActivationFunctionType.Tanh)
-
-        zeros = held.tile([D, BANK], BF16, name="zeros")
-        nc.vector.memset(zeros[:], 0.0)
-        unused_ps = psum.tile([D, BANK], F32, name="unused_ps")
-        for _ in range(WARMING_MATMULS):
-            nc.tensor.matmul(unused_ps[:], zeros[:, 0:D], zeros[:], start=True, stop=True)
 
         identity = held.tile([D, D], BF16, name="identity")
         make_identity(nc, identity[:])

@@ -7,6 +7,9 @@ D = 128
 V = 256
 N = 128
 
+BANK = 512
+WARMING_MATMULS = 3
+
 FLOPS = 2 * D * D * N + 2 * D * N * N
 
 
@@ -28,6 +31,12 @@ def tile_neuronsv2textclassifier_kernel(tc, table, w1, fw1, b1, mask, offs, out)
         nc.sync.dma_start(mask_f32[:], mask)
         b1_sb = held.tile([D, 1], F32, name="b1_sb")
         nc.scalar.dma_start(b1_sb[:], b1)
+
+        zeros = held.tile([D, BANK], BF16, name="zeros")
+        nc.vector.memset(zeros[:], 0.0)
+        unused_ps = psum.tile([D, BANK], F32, name="unused_ps")
+        for _ in range(WARMING_MATMULS):
+            nc.tensor.matmul(unused_ps[:], zeros[:, 0:D], zeros[:], start=True, stop=True)
 
         scratch = held.tile([D, 1], F32, name="scratch")
         nc.vector.memset(scratch[:], 0.0)

@@ -53,8 +53,8 @@ def tile_neuronsv2textclassifier_kernel(tc, table, w1, fw1, b1, mask, offs, out)
         y_bf = held.tile([D, N], BF16, name="y_bf")
         nc.vector.tensor_copy(y_bf[:], y_ps[:])
 
-        yT_ps = psum.tile([N, D], BF16, name="yT_ps")
-        nc.tensor.transpose(yT_ps[:], y_bf[:], identity[:])
+        yT_ps = psum.tile([N, D], F32, name="yT_ps")
+        nc.tensor.matmul(yT_ps[:], y_bf[:], identity[:], start=True, stop=True)
         mask_bf = held.tile([N, N], BF16, name="mask_bf")
         nc.vector.tensor_copy(mask_bf[:], mask_f32[:])
         yT_bf = held.tile([N, D], BF16, name="yT_bf")

@@ -53,7 +53,7 @@ def tile_neuronsv2textclassifier_kernel(tc, table, w1, fw1, b1, mask, offs, out)
         y_bf = held.tile([D, N], BF16, name="y_bf")
         nc.vector.tensor_copy(y_bf[:], y_ps[:])
 
-        yT_ps = psum.tile([N, D], F32, name="yT_ps")
+        yT_ps = psum.tile([N, D], BF16, name="yT_ps")
         nc.tensor.matmul(yT_ps[:], y_bf[:], identity[:], start=True, stop=True)
         mask_bf = held.tile([N, N], BF16, name="mask_bf")
         nc.vector.tensor_copy(mask_bf[:], mask_f32[:])

@@ -53,18 +53,30 @@ def tile_neuronsv2textclassifier_kernel(tc, table, w1, fw1, b1, mask, offs, out)
         y_bf = held.tile([D, N], BF16, name="y_bf")
         nc.vector.tensor_copy(y_bf[:], y_ps[:])
 
-        yT_ps = psum.tile([N, D], BF16, name="yT_ps")
-        nc.tensor.matmul(yT_ps[:], y_bf[:], identity[:], start=True, stop=True)
+        half = N // 2
+        yT_halves = []
+        for h in range(2):
+            yT_ps = psum.tile([N, half], BF16, name=f"yT{h}_ps")
+            nc.tensor.matmul(
+                yT_ps[:], y_bf[:], identity[:, h * half : (h + 1) * half], start=True, stop=True
+            )
+            yT_halves.append(yT_ps)
         mask_bf = held.tile([N, N], BF16, name="mask_bf")
         nc.vector.tensor_copy(mask_bf[:], mask_f32[:])
         yT_bf = held.tile([N, D], BF16, name="yT_bf")
-        nc.vector.tensor_copy(yT_bf[:], yT_ps[:])
-
-        mixed_ps = psum.tile([D, N], F32, name="mixed_ps")
-        nc.tensor.matmul(mixed_ps[:], yT_bf[:], mask_bf[:], start=True, stop=True)
+        for h in range(2):
+            nc.vector.tensor_copy(yT_bf[:, h * half : (h + 1) * half], yT_halves[h][:])
 
         out_sb = held.tile([D, N], F32, name="out_sb")
-        nc.scalar.activation(
-            out_sb[:], mixed_ps[:], mybir.ActivationFunctionType.Tanh, bias=b1_sb[:], scale=1.0 / N
-        )
+        for h in range(2):
+            positions = slice(h * half, (h + 1) * half)
+            mixed_ps = psum.tile([D, half], F32, name=f"mixed{h}_ps")
+            nc.tensor.matmul(mixed_ps[:], yT_bf[:], mask_bf[:, positions], start=True, stop=True)
+            nc.scalar.activation(
+                out_sb[:, positions],
+                mixed_ps[:],
+                mybir.ActivationFunctionType.Tanh,
+                bias=b1_sb[:],
+                scale=1.0 / N,
+            )
         nc.sync.dma_start(out, out_sb[:])

@@ -38,12 +38,11 @@ def tile_neuronsv2textclassifier_kernel(tc, table, w1, fw1, b1, mask, offs, out)
         for _ in range(WARMING_MATMULS):
             nc.tensor.matmul(unused_ps[:], zeros[:, 0:D], zeros[:], start=True, stop=True)
 
-        scratch = held.tile([D, 1], F32, name="scratch")
-        nc.vector.memset(scratch[:], 0.0)
-        nc.scalar.activation(scratch[:], scratch[:], mybir.ActivationFunctionType.Tanh)
-
         identity = held.tile([D, D], BF16, name="identity")
         make_identity(nc, identity[:])
+
+        mask_bf = held.tile([N, N], BF16, name="mask_bf")
+        nc.scalar.copy(mask_bf[:], mask_f32[:])
 
         w_sum = held.tile([D, D], BF16, name="w_sum")
         nc.vector.tensor_tensor(w_sum[:], w1_sb[:], fw1_sb[:], mybir.AluOpType.add)
@@ -61,8 +60,6 @@ def tile_neuronsv2textclassifier_kernel(tc, table, w1, fw1, b1, mask, offs, out)
                 yT_ps[:], y_bf[:], identity[:, h * half : (h + 1) * half], start=True, stop=True
             )
             yT_halves.append(yT_ps)
-        mask_bf = held.tile([N, N], BF16, name="mask_bf")
-        nc.vector.tensor_copy(mask_bf[:], mask_f32[:])
         yT_bf = held.tile([N, D], BF16, name="yT_bf")
         for h in range(2):
             nc.vector.tensor_copy(yT_bf[:, h * half : (h + 1) * half], yT_halves[h][:])

import concourse.mybir as mybir
from concourse.masks import make_identity

BF16, F32, U16 = mybir.dt.bfloat16, mybir.dt.float32, mybir.dt.uint16

D = 128
V = 256
N = 128

BANK = 512
WARMING_MATMULS = 3

FLOPS = 2 * D * D * N + 2 * D * N * N


def tile_neuronsv2textclassifier_kernel(tc, table, w1, fw1, b1, mask, offs, out):
    nc = tc.nc
    with (
        tc.tile_pool(name="held", bufs=1) as held,
        tc.psum_pool(name="psum", bufs=1) as psum,
    ):
        w1_sb = held.tile([D, D], BF16, name="w1_sb")
        nc.scalar.dma_start(w1_sb[:], w1)
        fw1_sb = held.tile([D, D], BF16, name="fw1_sb")
        nc.sync.dma_start(fw1_sb[:], fw1)
        table_sb = held.tile([D, V], BF16, name="table_sb")
        nc.scalar.dma_start(table_sb[:], table)
        offsets = held.tile([D, N // 16], U16, name="offsets")
        nc.sync.dma_start(offsets[:], offs)
        mask_f32 = held.tile([N, N], F32, name="mask_f32")
        nc.sync.dma_start(mask_f32[:], mask)
        b1_sb = held.tile([D, 1], F32, name="b1_sb")
        nc.scalar.dma_start(b1_sb[:], b1)

        zeros = held.tile([D, BANK], BF16, name="zeros")
        nc.vector.memset(zeros[:], 0.0)
        unused_ps = psum.tile([D, BANK], F32, name="unused_ps")
        for _ in range(WARMING_MATMULS):
            nc.tensor.matmul(unused_ps[:], zeros[:, 0:D], zeros[:], start=True, stop=True)

        identity = held.tile([D, D], BF16, name="identity")
        make_identity(nc, identity[:])

        mask_bf = held.tile([N, N], BF16, name="mask_bf")
        nc.scalar.copy(mask_bf[:], mask_f32[:])

        w_sum = held.tile([D, D], BF16, name="w_sum")
        nc.vector.tensor_tensor(w_sum[:], w1_sb[:], fw1_sb[:], mybir.AluOpType.add)

        y_ps = psum.tile([D, N], F32, name="y_ps")
        nc.tensor.matmul(y_ps[:], w_sum[:], table_sb[:].indirect(offsets[:]), start=True, stop=True)
        y_bf = held.tile([D, N], BF16, name="y_bf")
        nc.vector.tensor_copy(y_bf[:], y_ps[:])

        half = N // 2
        yT_halves = []
        for h in range(2):
            yT_ps = psum.tile([N, half], BF16, name=f"yT{h}_ps")
            nc.tensor.matmul(
                yT_ps[:], y_bf[:], identity[:, h * half : (h + 1) * half], start=True, stop=True
            )
            yT_halves.append(yT_ps)
        yT_bf = held.tile([N, D], BF16, name="yT_bf")
        for h in range(2):
            nc.vector.tensor_copy(yT_bf[:, h * half : (h + 1) * half], yT_halves[h][:])

        out_sb = held.tile([D, N], F32, name="out_sb")
        for h in range(2):
            positions = slice(h * half, (h + 1) * half)
            mixed_ps = psum.tile([D, half], F32, name=f"mixed{h}_ps")
            nc.tensor.matmul(mixed_ps[:], yT_bf[:], mask_bf[:, positions], start=True, stop=True)
            nc.scalar.activation(
                out_sb[:, positions],
                mixed_ps[:],
                mybir.ActivationFunctionType.Tanh,
                bias=b1_sb[:],
                scale=1.0 / N,
            )
        nc.sync.dma_start(out, out_sb[:])
